import numpy as np
import ml_dtypes


def mxq(x, axis, fmt="e4m3"):
    dtype, down = {"e4m3": (ml_dtypes.float8_e4m3fn, 7), "e5m2": (ml_dtypes.float8_e5m2, 14)}[fmt]
    v = np.moveaxis(np.asarray(x, np.float32).astype(ml_dtypes.bfloat16).astype(np.float64), axis, -1)
    blocks = v.reshape(v.shape[:-1] + (-1, 32))
    amax = np.abs(blocks).max(-1, keepdims=True)
    byte = np.maximum(np.where(amax > 0, np.frexp(amax)[1] - 1 + 127, 0) - down, 1)
    scale = np.exp2(byte - 127.0)
    codes = (blocks / scale).astype(np.float32).astype(dtype).astype(np.float64)
    return np.moveaxis((codes * scale).reshape(v.shape), -1, axis)


WIDE = False


def mx_kscale(k):
    if not WIDE:
        return np.ones(k)
    levels = np.array([10, -10, 5, -5, 0])
    if k % 512:
        return np.exp2(np.random.permutation(np.resize(levels, k // 32))).repeat(32)
    a = np.empty((k // 512, 16))
    for p in range(k // 512):
        a[p, :8] = np.random.permutation(np.resize(levels, 8))
        for g in range(8):
            far = levels[np.abs(levels - a[p, g]) >= 10]
            a[p, g + 8] = far[np.random.randint(len(far))]
    return np.exp2(a.ravel()).repeat(32)


BF16 = ml_dtypes.bfloat16


def bf(x):
    return np.asarray(x, np.float32).astype(BF16)


def f64(x):
    return np.asarray(x).astype(np.float64)


B, CIN, COUT, T, R, C = 2, 512, 512, 4, 4, 4


def setup_inputs():
    s = mx_kscale(CIN)
    x = np.random.standard_normal((B, CIN, T, R, C)) * s[None, :, None, None, None]
    W = np.random.standard_normal((7 * COUT, CIN)) * 0.5 / np.sqrt(CIN) / s[None, :]
    return {"x": bf(x), "W": bf(W)}


def _shift(a, axis, d):
    pads = [(0, 0)] * a.ndim
    idx = [slice(None)] * a.ndim
    if d > 0:
        pads[axis] = (1, 0)
        idx[axis] = slice(0, -1)
    else:
        pads[axis] = (0, 1)
        idx[axis] = slice(1, None)
    return np.pad(a, pads)[tuple(idx)]


def reference(x, W):
    cout = W.shape[0] // 7
    xq = mxq(f64(x), 1, "e4m3")
    Wq = mxq(f64(W), 1, "e4m3")
    all_out = xq.transpose(0, 2, 3, 4, 1) @ Wq.T
    a = all_out.reshape(*all_out.shape[:4], 7, cout)
    out = a[..., 0, :]
    out = out + _shift(a[..., 1, :], 1, +1)
    out = out + _shift(a[..., 2, :], 1, -1)
    out = out + _shift(a[..., 3, :], 2, +1)
    out = out + _shift(a[..., 4, :], 2, -1)
    out = out + _shift(a[..., 5, :], 3, +1)
    out = out + _shift(a[..., 6, :], 3, -1)
    return np.transpose(out, (0, 4, 1, 2, 3))

@@ -1,0 +1,149 @@
+from contextlib import ExitStack
+
+import concourse.masks as masks
+import concourse.mybir as mybir
+
+BF16 = mybir.dt.bfloat16
+F32 = mybir.dt.float32
+U32 = mybir.dt.uint32
+U8 = mybir.dt.uint8
+I32 = mybir.dt.int32
+FP8X4 = mybir.dt.float8_e4m3fn_x4
+
+P = 128
+LANES = 4
+BATCH = 2
+CHANNELS_IN = 512
+CHANNELS_OUT = 512
+SIDE = 4
+VOXELS = SIDE * SIDE * SIDE
+TOKENS = BATCH * VOXELS
+DIRECTIONS = 7
+OUT_TILES = CHANNELS_OUT // P
+HALVES = 2
+EVEN_PIECES = ((0, 2), (2, 2))
+TAPERED_PIECES = ((0, 2), (2, 1), (3, 1))
+RUN = 2
+VECTOR_EVERY = 4
+assert (DIRECTIONS - 1) % RUN == 0
+
+FLOPS = 2 * TOKENS * CHANNELS_IN * DIRECTIONS * CHANNELS_OUT
+
+
+def tile_stackeddirectionalconv3d_s_kernel(tc, x, W, out):
+    nc = tc.nc
+    with ExitStack() as ctx:
+        keep = ctx.enter_context(tc.tile_pool(name="keep", bufs=1))
+        w_pool = ctx.enter_context(tc.tile_pool(name="w_pool", bufs=DIRECTIONS))
+        acc_pool = ctx.enter_context(tc.psum_pool(name="acc_pool", bufs=1))
+        bank_pool = ctx.enter_context(tc.psum_pool(name="bank_pool", bufs=RUN * len(EVEN_PIECES)))
+        ctx.enter_context(tc.manual_schedule())
+
+        x_raw = keep.tile([P, BATCH * LANES * VOXELS], BF16)
+        nc.sync.dma_start(
+            out=x_raw[:].rearrange("q (b w) -> q b w", b=BATCH),
+            in_=x.rearrange("b (q i) t r c -> b q (i t r c)", q=P).rearrange("b q w -> q b w"),
+        )
+        w_rows = W.rearrange("(d p j) k -> d p (j k)", d=DIRECTIONS, p=P)
+        w_raw = []
+        for d in range(DIRECTIONS):
+            w_raw_d = w_pool.tile([P, OUT_TILES * CHANNELS_IN], BF16, name="w_raw")
+            for first_tile, tiles in TAPERED_PIECES if d == DIRECTIONS - 1 else ((0, OUT_TILES),):
+                columns = slice(first_tile * CHANNELS_IN, (first_tile + tiles) * CHANNELS_IN)
+                nc.sync.dma_start(out=w_raw_d[:, columns], in_=w_rows[d, :, columns])
+            w_raw.append(w_raw_d)
+
+        identity = keep.tile([P, P], F32)
+        masks.make_identity(nc, identity[:])
+
+        x_moved = keep.tile([P, DIRECTIONS, TOKENS * LANES], BF16, align_bytes=64)
+        x_codes = keep.tile([P, DIRECTIONS, TOKENS], U32, align_bytes=64)
+        x_scales = keep.tile([P, DIRECTIONS, TOKENS], U8, align_bytes=64)
+        nc.vector.memset(x_moved[:, 1:, :].bitcast(I32), 0)
+        nc.vector.tensor_copy(
+            out=x_moved[:, 0, :].rearrange("q (b v i) -> q b v i", b=BATCH, i=LANES),
+            in_=x_raw[:].rearrange("q (b i v) -> q b v i", b=BATCH, i=LANES),
+        )
+        for d in range(1, DIRECTIONS):
+            axis = (d - 1) // 2
+            step = SIDE ** (2 - axis) * LANES
+            period = SIDE * step
+            target = x_moved[:, d, :].rearrange("q (o w) -> q o w", w=period)
+            source = x_moved[:, 0, :].rearrange("q (o w) -> q o w", w=period)
+            if d % 2 == 1:
+                nc.vector.tensor_copy(out=target[:, :, step:], in_=source[:, :, : period - step])
+            else:
+                nc.vector.tensor_copy(out=target[:, :, : period - step], in_=source[:, :, step:])
+        for d in range(DIRECTIONS):
+            nc.vector.quantize_mx(
+                out=x_codes[:, d, :].bitcast(FP8X4), scales=x_scales[:, d, :], in_=x_moved[:, d, :]
+            )
+
+        w_codes = keep.tile([P, DIRECTIONS, CHANNELS_OUT], U32, align_bytes=64)
+        w_scales = keep.tile([P, DIRECTIONS, CHANNELS_OUT], U8, align_bytes=64)
+        acc = [acc_pool.tile([P, TOKENS], F32, name="acc%d" % j) for j in range(OUT_TILES)]
+
+        def transpose_and_quantise(d):
+            pieces = TAPERED_PIECES if d == DIRECTIONS - 1 else EVEN_PIECES
+            w_words = w_raw[d][:].bitcast(F32)
+            w_grouped = w_pool.tile([P, CHANNELS_OUT * LANES], BF16, name="w_grouped", align_bytes=64)
+            w_grouped_words = w_grouped[:].bitcast(F32)
+            for i, (first_tile, tiles) in enumerate(pieces):
+                bank = bank_pool.tile([P, HALVES, tiles * P], F32, name="bank")
+                for jj in range(tiles):
+                    for u in range(HALVES):
+                        row = (first_tile + jj) * HALVES * P
+                        nc.tensor.transpose(
+                            bank[:, u, jj * P : (jj + 1) * P],
+                            w_words[:, row + u : row + HALVES * P : HALVES],
+                            identity[:],
+                        )
+                side_by_side = w_grouped_words[
+                    :, first_tile * P * HALVES : (first_tile + tiles) * P * HALVES
+                ].rearrange("q (c u) -> q c u", u=HALVES)
+                if (d * len(EVEN_PIECES) + i) % VECTOR_EVERY == VECTOR_EVERY - 1:
+                    nc.vector.tensor_copy(out=side_by_side, in_=bank[:].rearrange("q u c -> q c u"))
+                else:
+                    nc.scalar.copy(out=side_by_side, in_=bank[:].rearrange("q u c -> q c u"))
+            for first_tile, tiles in pieces:
+                columns = slice(first_tile * P, (first_tile + tiles) * P)
+                nc.vector.quantize_mx(
+                    out=w_codes[:, d, columns].bitcast(FP8X4),
+                    scales=w_scales[:, d, columns],
+                    in_=w_grouped[:, first_tile * P * LANES : (first_tile + tiles) * P * LANES],
+                )
+
+        def multiply(d):
+            for j in range(OUT_TILES):
+                nc.tensor.matmul_mx(
+                    out=acc[j][:],
+                    lhsT=w_codes[:, d, j * P : (j + 1) * P].bitcast(FP8X4),
+                    lhsT_scale=w_scales[:, d, j * P : (j + 1) * P],
+                    rhs=x_codes[:, d, :].bitcast(FP8X4),
+                    rhs_scale=x_scales[:, d, :],
+                    start=(d == 0),
+                    stop=(d == DIRECTIONS - 1),
+                )
+
+        transpose_and_quantise(0)
+        for first in range(1, DIRECTIONS, RUN):
+            for d in range(first, first + RUN):
+                transpose_and_quantise(d)
+            for d in range(max(first - RUN, 0), first):
+                multiply(d)
+        for d in range(DIRECTIONS - RUN, DIRECTIONS):
+            multiply(d)
+
+        result = keep.tile([P, BATCH, OUT_TILES, VOXELS], F32)
+        out_rows = out.rearrange("b (p j) t r c -> p b j (t r c)", j=OUT_TILES)
+        for first_tile, tiles in TAPERED_PIECES:
+            for j in range(first_tile, first_tile + tiles):
+                sums = acc[j][:].rearrange("p (b v) -> p b v", b=BATCH)
+                if j % 2 == 0:
+                    nc.scalar.copy(out=result[:, :, j, :], in_=sums)
+                else:
+                    nc.vector.tensor_copy(out=result[:, :, j, :], in_=sums)
+            nc.sync.dma_start(
+                out=out_rows[:, :, first_tile : first_tile + tiles, :],
+                in_=result[:, :, first_tile : first_tile + tiles, :],
+            )

@@ -21,6 +21,7 @@ TOKENS = BATCH * VOXELS
 DIRECTIONS = 7
 OUT_TILES = CHANNELS_OUT // P
 HALVES = 2
+FIRST_LOADS = ((0, 1), (1, 1), (2, 2))
 EVEN_PIECES = ((0, 2), (2, 2))
 TAPERED_PIECES = ((0, 2), (2, 1), (3, 1))
 RUN = 2
@@ -39,19 +40,21 @@ def tile_stackeddirectionalconv3d_s_kernel(tc, x, W, out):
         bank_pool = ctx.enter_context(tc.psum_pool(name="bank_pool", bufs=RUN * len(EVEN_PIECES)))
         ctx.enter_context(tc.manual_schedule())
 
-        x_raw = keep.tile([P, BATCH * LANES * VOXELS], BF16)
-        nc.sync.dma_start(
-            out=x_raw[:].rearrange("q (b w) -> q b w", b=BATCH),
-            in_=x.rearrange("b (q i) t r c -> b q (i t r c)", q=P).rearrange("b q w -> q b w"),
-        )
         w_rows = W.rearrange("(d p j) k -> d p (j k)", d=DIRECTIONS, p=P)
         w_raw = []
         for d in range(DIRECTIONS):
             w_raw_d = w_pool.tile([P, OUT_TILES * CHANNELS_IN], BF16, name="w_raw")
-            for first_tile, tiles in TAPERED_PIECES if d == DIRECTIONS - 1 else ((0, OUT_TILES),):
+            loads = {0: FIRST_LOADS, DIRECTIONS - 1: TAPERED_PIECES}.get(d, ((0, OUT_TILES),))
+            for first_tile, tiles in loads:
                 columns = slice(first_tile * CHANNELS_IN, (first_tile + tiles) * CHANNELS_IN)
                 nc.sync.dma_start(out=w_raw_d[:, columns], in_=w_rows[d, :, columns])
             w_raw.append(w_raw_d)
+            if d == 0:
+                x_raw = keep.tile([P, BATCH * LANES * VOXELS], BF16)
+                nc.sync.dma_start(
+                    out=x_raw[:].rearrange("q (b w) -> q b w", b=BATCH),
+                    in_=x.rearrange("b (q i) t r c -> b q (i t r c)", q=P).rearrange("b q w -> q b w"),
+                )
 
         identity = keep.tile([P, P], F32)
         masks.make_identity(nc, identity[:])

@@ -22,11 +22,12 @@ DIRECTIONS = 7
 OUT_TILES = CHANNELS_OUT // P
 HALVES = 2
 FIRST_LOADS = ((0, 1), (1, 1), (2, 2))
-EVEN_PIECES = ((0, 2), (2, 2))
-TAPERED_PIECES = ((0, 2), (2, 1), (3, 1))
-RUN = 2
-VECTOR_EVERY = 4
-assert (DIRECTIONS - 1) % RUN == 0
+PIECES = ((0, 2), (2, 2))
+PSUM_BANKS = 8
+VECTOR_EVERY, VECTOR_TURN = 4, 2
+SCALAR_MOVES = (4, 5, 6)
+QUANTISE_LAG = 2
+X_QUANTISES = ((0, 4), (4, 6), (6, 7))
 
 FLOPS = 2 * TOKENS * CHANNELS_IN * DIRECTIONS * CHANNELS_OUT
 
@@ -36,25 +37,24 @@ def tile_stackeddirectionalconv3d_s_kernel(tc, x, W, out):
     with ExitStack() as ctx:
         keep = ctx.enter_context(tc.tile_pool(name="keep", bufs=1))
         w_pool = ctx.enter_context(tc.tile_pool(name="w_pool", bufs=DIRECTIONS))
-        acc_pool = ctx.enter_context(tc.psum_pool(name="acc_pool", bufs=1))
-        bank_pool = ctx.enter_context(tc.psum_pool(name="bank_pool", bufs=RUN * len(EVEN_PIECES)))
+        bank_pool = ctx.enter_context(tc.psum_pool(name="bank_pool", bufs=PSUM_BANKS))
         ctx.enter_context(tc.manual_schedule())
 
         w_rows = W.rearrange("(d p j) k -> d p (j k)", d=DIRECTIONS, p=P)
         w_raw = []
         for d in range(DIRECTIONS):
             w_raw_d = w_pool.tile([P, OUT_TILES * CHANNELS_IN], BF16, name="w_raw")
-            loads = {0: FIRST_LOADS, DIRECTIONS - 1: TAPERED_PIECES}.get(d, ((0, OUT_TILES),))
+            loads = {0: FIRST_LOADS, DIRECTIONS - 1: PIECES}.get(d, ((0, OUT_TILES),))
             for first_tile, tiles in loads:
+                if d == 0 and first_tile == 2:
+                    x_raw = keep.tile([P, BATCH * LANES * VOXELS], BF16)
+                    nc.sync.dma_start(
+                        out=x_raw[:].rearrange("q (b w) -> q b w", b=BATCH),
+                        in_=x.rearrange("b (q i) t r c -> b q (i t r c)", q=P).rearrange("b q w -> q b w"),
+                    )
                 columns = slice(first_tile * CHANNELS_IN, (first_tile + tiles) * CHANNELS_IN)
                 nc.sync.dma_start(out=w_raw_d[:, columns], in_=w_rows[d, :, columns])
             w_raw.append(w_raw_d)
-            if d == 0:
-                x_raw = keep.tile([P, BATCH * LANES * VOXELS], BF16)
-                nc.sync.dma_start(
-                    out=x_raw[:].rearrange("q (b w) -> q b w", b=BATCH),
-                    in_=x.rearrange("b (q i) t r c -> b q (i t r c)", q=P).rearrange("b q w -> q b w"),
-                )
 
         identity = keep.tile([P, P], F32)
         masks.make_identity(nc, identity[:])
@@ -67,59 +67,89 @@ def tile_stackeddirectionalconv3d_s_kernel(tc, x, W, out):
             out=x_moved[:, 0, :].rearrange("q (b v i) -> q b v i", b=BATCH, i=LANES),
             in_=x_raw[:].rearrange("q (b i v) -> q b v i", b=BATCH, i=LANES),
         )
-        for d in range(1, DIRECTIONS):
+
+        def move(d):
             axis = (d - 1) // 2
             step = SIDE ** (2 - axis) * LANES
             period = SIDE * step
             target = x_moved[:, d, :].rearrange("q (o w) -> q o w", w=period)
             source = x_moved[:, 0, :].rearrange("q (o w) -> q o w", w=period)
+            copy = nc.scalar.copy if d in SCALAR_MOVES else nc.vector.tensor_copy
             if d % 2 == 1:
-                nc.vector.tensor_copy(out=target[:, :, step:], in_=source[:, :, : period - step])
+                copy(out=target[:, :, step:], in_=source[:, :, : period - step])
             else:
-                nc.vector.tensor_copy(out=target[:, :, : period - step], in_=source[:, :, step:])
-        for d in range(DIRECTIONS):
+                copy(out=target[:, :, : period - step], in_=source[:, :, step:])
+
+        def quantise_x(first, end):
             nc.vector.quantize_mx(
-                out=x_codes[:, d, :].bitcast(FP8X4), scales=x_scales[:, d, :], in_=x_moved[:, d, :]
+                out=x_codes[:, first:end, :].rearrange("q d c -> q (d c)").bitcast(FP8X4),
+                scales=x_scales[:, first:end, :].rearrange("q d c -> q (d c)"),
+                in_=x_moved[:, first:end, :].rearrange("q d c -> q (d c)"),
             )
 
         w_codes = keep.tile([P, DIRECTIONS, CHANNELS_OUT], U32, align_bytes=64)
         w_scales = keep.tile([P, DIRECTIONS, CHANNELS_OUT], U8, align_bytes=64)
-        acc = [acc_pool.tile([P, TOKENS], F32, name="acc%d" % j) for j in range(OUT_TILES)]
+        w_grouped = [w_pool.tile([P, CHANNELS_OUT * LANES], BF16, name="w_grouped", align_bytes=64) for d in range(DIRECTIONS)]
 
-        def transpose_and_quantise(d):
-            pieces = TAPERED_PIECES if d == DIRECTIONS - 1 else EVEN_PIECES
+        pieces = [(d, first_tile, tiles) for d in range(DIRECTIONS) for first_tile, tiles in PIECES]
+
+        def transpose(d, first_tile, tiles):
             w_words = w_raw[d][:].bitcast(F32)
-            w_grouped = w_pool.tile([P, CHANNELS_OUT * LANES], BF16, name="w_grouped", align_bytes=64)
-            w_grouped_words = w_grouped[:].bitcast(F32)
-            for i, (first_tile, tiles) in enumerate(pieces):
-                bank = bank_pool.tile([P, HALVES, tiles * P], F32, name="bank")
-                for jj in range(tiles):
-                    for u in range(HALVES):
-                        row = (first_tile + jj) * HALVES * P
-                        nc.tensor.transpose(
-                            bank[:, u, jj * P : (jj + 1) * P],
-                            w_words[:, row + u : row + HALVES * P : HALVES],
-                            identity[:],
-                        )
-                side_by_side = w_grouped_words[
-                    :, first_tile * P * HALVES : (first_tile + tiles) * P * HALVES
-                ].rearrange("q (c u) -> q c u", u=HALVES)
-                if (d * len(EVEN_PIECES) + i) % VECTOR_EVERY == VECTOR_EVERY - 1:
-                    nc.vector.tensor_copy(out=side_by_side, in_=bank[:].rearrange("q u c -> q c u"))
-                else:
-                    nc.scalar.copy(out=side_by_side, in_=bank[:].rearrange("q u c -> q c u"))
-            for first_tile, tiles in pieces:
-                columns = slice(first_tile * P, (first_tile + tiles) * P)
-                nc.vector.quantize_mx(
-                    out=w_codes[:, d, columns].bitcast(FP8X4),
-                    scales=w_scales[:, d, columns],
-                    in_=w_grouped[:, first_tile * P * LANES : (first_tile + tiles) * P * LANES],
-                )
+            bank = bank_pool.tile([P, HALVES, tiles * P], F32, name="bank")
+            for jj in range(tiles):
+                for u in range(HALVES):
+                    row = (first_tile + jj) * HALVES * P
+                    nc.tensor.transpose(
+                        bank[:, u, jj * P : (jj + 1) * P],
+                        w_words[:, row + u : row + HALVES * P : HALVES],
+                        identity[:],
+                    )
+            return bank
 
-        def multiply(d):
-            for j in range(OUT_TILES):
+        def regroup(n, bank):
+            d, first_tile, tiles = pieces[n]
+            side_by_side = (
+                w_grouped[d][:]
+                .bitcast(F32)[:, first_tile * P * HALVES : (first_tile + tiles) * P * HALVES]
+                .rearrange("q (c u) -> q c u", u=HALVES)
+            )
+            copy = nc.vector.tensor_copy if n % VECTOR_EVERY == VECTOR_TURN else nc.scalar.copy
+            copy(out=side_by_side, in_=bank[:].rearrange("q u c -> q c u"))
+
+        def quantise_w(n):
+            d, first_tile, tiles = pieces[n]
+            columns = slice(first_tile * P, (first_tile + tiles) * P)
+            nc.vector.quantize_mx(
+                out=w_codes[:, d, columns].bitcast(FP8X4),
+                scales=w_scales[:, d, columns],
+                in_=w_grouped[d][:, first_tile * P * LANES : (first_tile + tiles) * P * LANES],
+            )
+
+        for d in range(1, DIRECTIONS):
+            if d not in SCALAR_MOVES:
+                move(d)
+        quantise_x(*X_QUANTISES[0])
+        for n, piece in enumerate(pieces):
+            if n >= QUANTISE_LAG:
+                quantise_w(n - QUANTISE_LAG)
+            regroup(n, transpose(*piece))
+            if piece[0] == 0 and n == len(PIECES) - 1:
+                for d in SCALAR_MOVES:
+                    move(d)
+            if n == 2 * len(PIECES) - 1:
+                for first, end in X_QUANTISES[1:]:
+                    quantise_x(first, end)
+        for n in range(len(pieces) - QUANTISE_LAG, len(pieces)):
+            quantise_w(n)
+
+        result = keep.tile([P, BATCH, OUT_TILES, VOXELS], F32)
+        out_rows = out.rearrange("b (p j) t r c -> p b j (t r c)", j=OUT_TILES)
+        acc = [bank_pool.tile([P, HALVES, 2 * P], F32, name="bank") for j in range(OUT_TILES)]
+
+        def multiply(j, directions):
+            for d in directions:
                 nc.tensor.matmul_mx(
-                    out=acc[j][:],
+                    out=acc[j][:, 0, :TOKENS],
                     lhsT=w_codes[:, d, j * P : (j + 1) * P].bitcast(FP8X4),
                     lhsT_scale=w_scales[:, d, j * P : (j + 1) * P],
                     rhs=x_codes[:, d, :].bitcast(FP8X4),
@@ -128,25 +158,26 @@ def tile_stackeddirectionalconv3d_s_kernel(tc, x, W, out):
                     stop=(d == DIRECTIONS - 1),
                 )
 
-        transpose_and_quantise(0)
-        for first in range(1, DIRECTIONS, RUN):
-            for d in range(first, first + RUN):
-                transpose_and_quantise(d)
-            for d in range(max(first - RUN, 0), first):
-                multiply(d)
-        for d in range(DIRECTIONS - RUN, DIRECTIONS):
-            multiply(d)
+        def copy_out(j):
+            sums = acc[j][:, 0, :TOKENS].rearrange("p (b v) -> p b v", b=BATCH)
+            if j % 2 == 0:
+                nc.scalar.copy(out=result[:, :, j, :], in_=sums)
+            else:
+                nc.vector.tensor_copy(out=result[:, :, j, :], in_=sums)
 
-        result = keep.tile([P, BATCH, OUT_TILES, VOXELS], F32)
-        out_rows = out.rearrange("b (p j) t r c -> p b j (t r c)", j=OUT_TILES)
-        for first_tile, tiles in TAPERED_PIECES:
-            for j in range(first_tile, first_tile + tiles):
-                sums = acc[j][:].rearrange("p (b v) -> p b v", b=BATCH)
-                if j % 2 == 0:
-                    nc.scalar.copy(out=result[:, :, j, :], in_=sums)
-                else:
-                    nc.vector.tensor_copy(out=result[:, :, j, :], in_=sums)
+        def store(first_tile, tiles):
             nc.sync.dma_start(
                 out=out_rows[:, :, first_tile : first_tile + tiles, :],
                 in_=result[:, :, first_tile : first_tile + tiles, :],
             )
+
+        for j in (0, 1):
+            multiply(j, range(DIRECTIONS - 1))
+        for j in (0, 1):
+            multiply(j, (DIRECTIONS - 1,))
+            copy_out(j)
+        store(0, 2)
+        for j in (2, 3):
+            multiply(j, range(DIRECTIONS))
+            copy_out(j)
+            store(j, 1)

from contextlib import ExitStack

import concourse.masks as masks
import concourse.mybir as mybir

BF16 = mybir.dt.bfloat16
F32 = mybir.dt.float32
U32 = mybir.dt.uint32
U8 = mybir.dt.uint8
I32 = mybir.dt.int32
FP8X4 = mybir.dt.float8_e4m3fn_x4

P = 128
LANES = 4
BATCH = 2
CHANNELS_IN = 512
CHANNELS_OUT = 512
SIDE = 4
VOXELS = SIDE * SIDE * SIDE
TOKENS = BATCH * VOXELS
DIRECTIONS = 7
OUT_TILES = CHANNELS_OUT // P
HALVES = 2
FIRST_LOADS = ((0, 1), (1, 1), (2, 2))
PIECES = ((0, 2), (2, 2))
PSUM_BANKS = 8
VECTOR_EVERY, VECTOR_TURN = 4, 2
SCALAR_MOVES = (4, 5, 6)
QUANTISE_LAG = 2
X_QUANTISES = ((0, 4), (4, 6), (6, 7))

FLOPS = 2 * TOKENS * CHANNELS_IN * DIRECTIONS * CHANNELS_OUT


def tile_stackeddirectionalconv3d_s_kernel(tc, x, W, out):
    nc = tc.nc
    with ExitStack() as ctx:
        keep = ctx.enter_context(tc.tile_pool(name="keep", bufs=1))
        w_pool = ctx.enter_context(tc.tile_pool(name="w_pool", bufs=DIRECTIONS))
        bank_pool = ctx.enter_context(tc.psum_pool(name="bank_pool", bufs=PSUM_BANKS))
        ctx.enter_context(tc.manual_schedule())

        w_rows = W.rearrange("(d p j) k -> d p (j k)", d=DIRECTIONS, p=P)
        w_raw = []
        for d in range(DIRECTIONS):
            w_raw_d = w_pool.tile([P, OUT_TILES * CHANNELS_IN], BF16, name="w_raw")
            loads = {0: FIRST_LOADS, DIRECTIONS - 1: PIECES}.get(d, ((0, OUT_TILES),))
            for first_tile, tiles in loads:
                if d == 0 and first_tile == 2:
                    x_raw = keep.tile([P, BATCH * LANES * VOXELS], BF16)
                    nc.sync.dma_start(
                        out=x_raw[:].rearrange("q (b w) -> q b w", b=BATCH),
                        in_=x.rearrange("b (q i) t r c -> b q (i t r c)", q=P).rearrange("b q w -> q b w"),
                    )
                columns = slice(first_tile * CHANNELS_IN, (first_tile + tiles) * CHANNELS_IN)
                nc.sync.dma_start(out=w_raw_d[:, columns], in_=w_rows[d, :, columns])
            w_raw.append(w_raw_d)

        identity = keep.tile([P, P], F32)
        masks.make_identity(nc, identity[:])

        x_moved = keep.tile([P, DIRECTIONS, TOKENS * LANES], BF16, align_bytes=64)
        x_codes = keep.tile([P, DIRECTIONS, TOKENS], U32, align_bytes=64)
        x_scales = keep.tile([P, DIRECTIONS, TOKENS], U8, align_bytes=64)
        nc.vector.memset(x_moved[:, 1:, :].bitcast(I32), 0)
        nc.vector.tensor_copy(
            out=x_moved[:, 0, :].rearrange("q (b v i) -> q b v i", b=BATCH, i=LANES),
            in_=x_raw[:].rearrange("q (b i v) -> q b v i", b=BATCH, i=LANES),
        )

        def move(d):
            axis = (d - 1) // 2
            step = SIDE ** (2 - axis) * LANES
            period = SIDE * step
            target = x_moved[:, d, :].rearrange("q (o w) -> q o w", w=period)
            source = x_moved[:, 0, :].rearrange("q (o w) -> q o w", w=period)
            copy = nc.scalar.copy if d in SCALAR_MOVES else nc.vector.tensor_copy
            if d % 2 == 1:
                copy(out=target[:, :, step:], in_=source[:, :, : period - step])
            else:
                copy(out=target[:, :, : period - step], in_=source[:, :, step:])

        def quantise_x(first, end):
            nc.vector.quantize_mx(
                out=x_codes[:, first:end, :].rearrange("q d c -> q (d c)").bitcast(FP8X4),
                scales=x_scales[:, first:end, :].rearrange("q d c -> q (d c)"),
                in_=x_moved[:, first:end, :].rearrange("q d c -> q (d c)"),
            )

        w_codes = keep.tile([P, DIRECTIONS, CHANNELS_OUT], U32, align_bytes=64)
        w_scales = keep.tile([P, DIRECTIONS, CHANNELS_OUT], U8, align_bytes=64)
        w_grouped = [w_pool.tile([P, CHANNELS_OUT * LANES], BF16, name="w_grouped", align_bytes=64) for d in range(DIRECTIONS)]

        pieces = [(d, first_tile, tiles) for d in range(DIRECTIONS) for first_tile, tiles in PIECES]

        def transpose(d, first_tile, tiles):
            w_words = w_raw[d][:].bitcast(F32)
            bank = bank_pool.tile([P, HALVES, tiles * P], F32, name="bank")
            for jj in range(tiles):
                for u in range(HALVES):
                    row = (first_tile + jj) * HALVES * P
                    nc.tensor.transpose(
                        bank[:, u, jj * P : (jj + 1) * P],
                        w_words[:, row + u : row + HALVES * P : HALVES],
                        identity[:],
                    )
            return bank

        def regroup(n, bank):
            d, first_tile, tiles = pieces[n]
            side_by_side = (
                w_grouped[d][:]
                .bitcast(F32)[:, first_tile * P * HALVES : (first_tile + tiles) * P * HALVES]
                .rearrange("q (c u) -> q c u", u=HALVES)
            )
            copy = nc.vector.tensor_copy if n % VECTOR_EVERY == VECTOR_TURN else nc.scalar.copy
            copy(out=side_by_side, in_=bank[:].rearrange("q u c -> q c u"))

        def quantise_w(n):
            d, first_tile, tiles = pieces[n]
            columns = slice(first_tile * P, (first_tile + tiles) * P)
            nc.vector.quantize_mx(
                out=w_codes[:, d, columns].bitcast(FP8X4),
                scales=w_scales[:, d, columns],
                in_=w_grouped[d][:, first_tile * P * LANES : (first_tile + tiles) * P * LANES],
            )

        for d in range(1, DIRECTIONS):
            if d not in SCALAR_MOVES:
                move(d)
        quantise_x(*X_QUANTISES[0])
        for n, piece in enumerate(pieces):
            if n >= QUANTISE_LAG:
                quantise_w(n - QUANTISE_LAG)
            regroup(n, transpose(*piece))
            if piece[0] == 0 and n == len(PIECES) - 1:
                for d in SCALAR_MOVES:
                    move(d)
            if n == 2 * len(PIECES) - 1:
                for first, end in X_QUANTISES[1:]:
                    quantise_x(first, end)
        for n in range(len(pieces) - QUANTISE_LAG, len(pieces)):
            quantise_w(n)

        result = keep.tile([P, BATCH, OUT_TILES, VOXELS], F32)
        out_rows = out.rearrange("b (p j) t r c -> p b j (t r c)", j=OUT_TILES)
        acc = [bank_pool.tile([P, HALVES, 2 * P], F32, name="bank") for j in range(OUT_TILES)]

        def multiply(j, directions):
            for d in directions:
                nc.tensor.matmul_mx(
                    out=acc[j][:, 0, :TOKENS],
                    lhsT=w_codes[:, d, j * P : (j + 1) * P].bitcast(FP8X4),
                    lhsT_scale=w_scales[:, d, j * P : (j + 1) * P],
                    rhs=x_codes[:, d, :].bitcast(FP8X4),
                    rhs_scale=x_scales[:, d, :],
                    start=(d == 0),
                    stop=(d == DIRECTIONS - 1),
                )

        def copy_out(j):
            sums = acc[j][:, 0, :TOKENS].rearrange("p (b v) -> p b v", b=BATCH)
            if j % 2 == 0:
                nc.scalar.copy(out=result[:, :, j, :], in_=sums)
            else:
                nc.vector.tensor_copy(out=result[:, :, j, :], in_=sums)

        def store(first_tile, tiles):
            nc.sync.dma_start(
                out=out_rows[:, :, first_tile : first_tile + tiles, :],
                in_=result[:, :, first_tile : first_tile + tiles, :],
            )

        for j in (0, 1):
            multiply(j, range(DIRECTIONS - 1))
        for j in (0, 1):
            multiply(j, (DIRECTIONS - 1,))
            copy_out(j)
        store(0, 2)
        for j in (2, 3):
            multiply(j, range(DIRECTIONS))
            copy_out(j)
            store(j, 1)
